import numpy as np
import ml_dtypes


def mxq(x, axis, fmt="e4m3"):
    dtype, down = {"e4m3": (ml_dtypes.float8_e4m3fn, 7), "e5m2": (ml_dtypes.float8_e5m2, 14)}[fmt]
    v = np.moveaxis(np.asarray(x, np.float32).astype(ml_dtypes.bfloat16).astype(np.float64), axis, -1)
    blocks = v.reshape(v.shape[:-1] + (-1, 32))
    amax = np.abs(blocks).max(-1, keepdims=True)
    byte = np.maximum(np.where(amax > 0, np.frexp(amax)[1] - 1 + 127, 0) - down, 1)
    scale = np.exp2(byte - 127.0)
    codes = (blocks / scale).astype(np.float32).astype(dtype).astype(np.float64)
    return np.moveaxis((codes * scale).reshape(v.shape), -1, axis)


WIDE = False


def mx_kscale(k):
    if not WIDE:
        return np.ones(k)
    levels = np.array([10, -10, 5, -5, 0])
    a = np.random.permutation(np.resize(levels, k // 512 * 4)).reshape(k // 512, 4)
    idx = np.arange(k)
    return np.exp2(a[idx // 512, idx % 128 // 32])


BF16 = ml_dtypes.bfloat16


def bf(x):
    return np.asarray(x, np.float32).astype(BF16)


def f64(x):
    return np.asarray(x).astype(np.float64)


B, K, N = 8192, 512, 512
EPS = 1e-7
MIN_NORM = 1e-15
MAX_TANH_ARG = 15.0


def _cosh(v):
    return 0.5 * (np.exp(v) + np.exp(-v))


def _sinh(v):
    return 0.5 * (np.exp(v) - np.exp(-v))


def _arccosh(v):
    return np.log(v + np.sqrt(v * v - 1.0))


def _norm(v):
    return np.sqrt(np.sum(v * v, axis=-1, keepdims=True))


def _mink_dot(u, v):
    return -u[..., :1] * v[..., :1] + np.sum(u[..., 1:] * v[..., 1:], axis=-1, keepdims=True)


def _proj(x):
    sp = x[..., 1:]
    t = np.sqrt(1.0 + np.sum(sp * sp, axis=-1, keepdims=True))
    return np.concatenate([t, sp], axis=-1)


def _proj_tan(u, x):
    ux = np.sum(x[..., 1:] * u[..., 1:], axis=-1, keepdims=True)
    t = ux / np.maximum(x[..., :1], MIN_NORM)
    return np.concatenate([t, u[..., 1:]], axis=-1)


def logmap_0(x):
    sp = x[..., 1:]
    n = np.maximum(_norm(sp), MIN_NORM)
    theta = np.maximum(x[..., :1], 1.0 + EPS)
    out_sp = _arccosh(theta) * sp / n
    return np.concatenate([np.zeros_like(theta), out_sp], axis=-1)


def expmap_0(u, backproject=True):
    sp = u[..., 1:]
    n = np.maximum(_norm(sp), MIN_NORM)
    theta = np.minimum(n, MAX_TANH_ARG)
    t = _cosh(theta)
    out_sp = _sinh(theta) * sp / n
    res = np.concatenate([t, out_sp], axis=-1)
    return _proj(res) if backproject else res


def ptransp_0(u, x):
    x0 = x[..., :1]
    y = x[..., 1:]
    y_norm = np.maximum(_norm(y), MIN_NORM)
    y_hat = y / y_norm
    v_time = -y_norm
    v_space = (1.0 - x0) * y_hat
    alpha = np.sum(y_hat * u[..., 1:], axis=-1, keepdims=True)
    res_time = np.zeros_like(x0) - alpha * v_time
    res_space = u[..., 1:] - alpha * v_space
    res = np.concatenate([res_time, res_space], axis=-1)
    return _proj_tan(res, x)


def expmap(u, x, backproject=True):
    unorm = np.sqrt(np.maximum(_mink_dot(u, u), MIN_NORM))
    theta = np.minimum(np.maximum(unorm, MIN_NORM), MAX_TANH_ARG)
    res = _cosh(theta) * x + _sinh(theta) * u / theta
    return _proj(res) if backproject else res


def setup_inputs():
    s = mx_kscale(K)
    c = np.sqrt(np.mean(s * s))
    sp = (np.random.standard_normal((B, K)) + 1.0) * (4.0 / np.sqrt(2.0 * K)) * (0.5 + np.random.random((B, 1)))
    sp = sp * s[None, :] / c
    t = np.sqrt(1.0 + np.sum(sp * sp, axis=-1, keepdims=True))
    w0 = np.random.standard_normal((N, K)) * (0.8 / np.sqrt(N))
    p = w0.sum(axis=1)
    b = 0.5 * np.random.standard_normal((1, N)) / np.sqrt(N) + 0.5 * p[None, :] / np.sqrt(np.sum(p * p))
    return {"x": bf(np.concatenate([t, sp], axis=-1)), "weight": bf(w0 / s[None, :] * c), "bias": bf(b)}


def reference(x, weight, bias):
    x, weight, bias = f64(x), f64(weight), f64(bias)
    u = logmap_0(x)
    h_sp = mxq(u[..., 1:], 1, "e4m3") @ mxq(weight, 1, "e4m3").T
    h = np.concatenate([np.zeros_like(h_sp[..., :1]), h_sp], axis=-1)
    m = expmap_0(h, backproject=True)
    b = np.concatenate([np.zeros_like(bias[..., :1]), bias], axis=-1)
    b = np.broadcast_to(b, m.shape)
    pt_b = ptransp_0(b, m)
    return expmap(pt_b, m, backproject=True)

@@ -1,0 +1,461 @@
+from contextlib import ExitStack
+
+import concourse.mybir as mybir
+from concourse.masks import make_identity
+
+F32 = mybir.dt.float32
+BF16 = mybir.dt.bfloat16
+U32 = mybir.dt.uint32
+U8 = mybir.dt.uint8
+FP8X4 = mybir.dt.float8_e4m3fn_x4
+ALU = mybir.AluOpType
+ACT = mybir.ActivationFunctionType
+
+P = 128
+PACK = 4
+ROWS = 8192
+K = 512
+N = 512
+WIDTH = K + 1
+TILES = ROWS // P
+PAIRS = TILES // 2
+GROUP = 4
+GROUP_PITCH = 2064
+CHUNK = 8
+GROUPS = TILES // GROUP
+CHUNKS = TILES // CHUNK
+PAIRS_IN_GROUP = GROUP // 2
+PAIRS_IN_CHUNK = CHUNK // 2
+
+NORM_LEAD = 8
+SCALE_LEAD = 3
+REGROUP_LEAD = 2
+QUANT_LEAD = 1
+DOT_LAG = 1
+LENGTH_LAG = 2
+EXP_LAG = 4
+FACTOR_LAG = 5
+OUT_LAG = 9
+FIRST_STEP = -NORM_LEAD
+LAST_STEP = PAIRS + OUT_LAG
+
+FLOPS = 2 * ROWS * K * N
+
+
+def tile_hyperboliclinearhyperboloid_t_kernel(tc, x, weight, bias, out):
+    nc = tc.nc
+    x_rows = x.rearrange("(p t) c -> p t c", t=TILES)
+    out_rows = out.rearrange("(p t) c -> p t c", t=TILES)
+
+    with ExitStack() as ctx:
+        ctx.enter_context(tc.manual_schedule())
+        keep = ctx.enter_context(tc.tile_pool(name="keep", bufs=1))
+        stage = ctx.enter_context(tc.tile_pool(name="stage", bufs=3))
+        unread = ctx.enter_context(tc.tile_pool(name="unread", bufs=4))
+        result = ctx.enter_context(tc.tile_pool(name="result", bufs=3))
+        psum_turned = ctx.enter_context(tc.psum_pool(name="psum_turned", bufs=2))
+        psum_first = ctx.enter_context(tc.psum_pool(name="psum_first", bufs=4))
+        psum_second = ctx.enter_context(tc.psum_pool(name="psum_second", bufs=2))
+
+        x_sb = keep.tile([P, GROUPS, GROUP_PITCH], BF16)
+        w_sb = keep.tile([P, PACK, K], BF16)
+        bias_bf = keep.tile([P, N], BF16)
+
+        def load_group(g):
+            tiles = slice(g * GROUP, (g + 1) * GROUP)
+            nc.sync.dma_start(
+                out=x_sb[:, g, 0 : GROUP * WIDTH], in_=x_rows[:, tiles, :].rearrange("p t c -> p (t c)")
+            )
+
+        def spatial(t):
+            first = (t % GROUP) * WIDTH
+            return x_sb[:, t // GROUP, first + 1 : first + WIDTH]
+
+        def time_coordinates(c):
+            groups = slice(c * CHUNK // GROUP, (c + 1) * CHUNK // GROUP)
+            return x_sb[:, groups, 0 : GROUP * WIDTH].rearrange("p g (t c) -> p g t c", c=WIDTH)[:, :, :, 0]
+
+        load_group(0)
+        nc.sync.dma_start(out=w_sb[:], in_=weight.rearrange("(i p) k -> p i k", p=P))
+        load_group(1)
+        load_group(2)
+        load_group(3)
+        nc.sync.dma_start(out=bias_bf[:], in_=bias.rearrange("o n -> (o n)").partition_broadcast(P))
+        for g in range(4, GROUPS):
+            load_group(g)
+
+        ident = keep.tile([P, P], BF16)
+        make_identity(nc, ident[:])
+        half = keep.tile([P, CHUNK], F32)
+        minus_half = keep.tile([P, CHUNK], F32)
+        nc.gpsimd.memset(half[:], 0.5)
+        nc.gpsimd.memset(minus_half[:], -0.5)
+
+        def row_values(name):
+            return keep.tile([P, TILES], F32, name=name)
+
+        above_one = row_values("above_one")
+        theta = row_values("theta")
+        root_arg = row_values("root_arg")
+        root = row_values("root")
+        log_arg = row_values("log_arg")
+        log_len = row_values("log_len")
+        norm_sq = row_values("norm_sq")
+        floor_sq = row_values("floor_sq")
+        norm_inv = row_values("norm_inv")
+        u_scale = row_values("u_scale")
+        h_sq = row_values("h_sq")
+        h_bias = row_values("h_bias")
+        r_sq = row_values("r_sq")
+        r_inv = row_values("r_inv")
+        r_len = row_values("r_len")
+        r_clamped = row_values("r_clamped")
+        grow = row_values("grow")
+        decay = row_values("decay")
+        d = row_values("d")
+        g2 = row_values("g2")
+        ca = row_values("ca")
+        ca_d = row_values("ca_d")
+        ca_g = row_values("ca_g")
+        d_over_r = row_values("d_over_r")
+        inner_a = row_values("inner_a")
+        inner_w = row_values("inner_w")
+        h_factor = row_values("h_factor")
+        w_less_ct = row_values("w_less_ct")
+        w_sq = row_values("w_sq")
+        time_sq = row_values("time_sq")
+        out_time = row_values("out_time")
+
+        def chunk_columns(c):
+            return slice(c * CHUNK, (c + 1) * CHUNK)
+
+        u_codes = keep.tile([P, TILES * P], U32, align_bytes=64)
+        u_scales = keep.tile([P, TILES * P], U8, align_bytes=64)
+        w_codes = keep.tile([P, N], U32, align_bytes=64)
+        w_scales = keep.tile([P, N], U8, align_bytes=64)
+
+        def turn(two_tiles):
+            turned = psum_turned.tile([P, 2 * PACK, P], BF16)
+            for e in range(2):
+                for j in range(PACK):
+                    nc.tensor.transpose(
+                        out=turned[:, e * PACK + j, :],
+                        in_=two_tiles[:, e, j * P : (j + 1) * P],
+                        identity=ident[:],
+                    )
+            return turned
+
+        def regroup(copy, turned):
+            grouped = stage.tile([P, 2 * P, PACK], BF16, align_bytes=64)
+            copy(
+                out=grouped[:].rearrange("p (e r) j -> p e r j", e=2),
+                in_=turned[:].rearrange("p (e j) r -> p e r j", e=2),
+            )
+            return grouped
+
+        def quantise(grouped, codes, scales):
+            nc.vector.quantize_mx(
+                out=codes.bitcast(FP8X4), scales=scales, in_=grouped[:].rearrange("p r j -> p (r j)")
+            )
+
+        def in_range(pair):
+            return 0 <= pair < PAIRS
+
+        def chunk_ended(pair):
+            if in_range(pair) and pair % PAIRS_IN_CHUNK == PAIRS_IN_CHUNK - 1:
+                return pair // PAIRS_IN_CHUNK
+            return None
+
+        def log_argument(c):
+            cols = chunk_columns(c)
+            nc.vector.tensor_scalar(
+                out=above_one[:, cols].rearrange("p (g t) -> p g t", t=GROUP), in0=time_coordinates(c),
+                scalar1=-1.0, scalar2=1e-7, op0=ALU.add, op1=ALU.max,
+            )
+            nc.vector.scalar_tensor_tensor(
+                out=root_arg[:, cols], in0=above_one[:, cols], scalar=2.0, in1=above_one[:, cols],
+                op0=ALU.add, op1=ALU.mult,
+            )
+            nc.vector.tensor_scalar(out=theta[:, cols], in0=above_one[:, cols], scalar1=1.0, scalar2=None, op0=ALU.add)
+            nc.gpsimd.tensor_tensor(out=root[:, cols], in0=root_arg[:, cols], in1=half[:], op=ALU.pow)
+            nc.gpsimd.tensor_tensor(out=log_arg[:, cols], in0=theta[:, cols], in1=root[:, cols], op=ALU.add)
+
+        def log_length(c):
+            cols = chunk_columns(c)
+            nc.scalar.activation(out=log_len[:, cols], in_=log_arg[:, cols], func=ACT.Ln)
+
+        def norm_square(pair):
+            if not in_range(pair):
+                return
+            for t in (2 * pair, 2 * pair + 1):
+                squares = unread.tile([P, K], BF16)
+                nc.scalar.activation(
+                    out=squares[:], in_=spatial(t), func=ACT.Square, accum_out=norm_sq[:, t : t + 1]
+                )
+
+        def scale_of_u(pair):
+            if not in_range(pair) or pair % PAIRS_IN_GROUP != 0:
+                return
+            cols = slice(2 * pair, 2 * pair + GROUP)
+            nc.gpsimd.tensor_scalar(
+                out=floor_sq[:, cols], in0=norm_sq[:, cols], scalar1=1e-30, scalar2=None, op0=ALU.max
+            )
+            nc.gpsimd.tensor_tensor(
+                out=norm_inv[:, cols], in0=floor_sq[:, cols], in1=minus_half[:, 0:GROUP], op=ALU.pow
+            )
+            nc.gpsimd.tensor_tensor(out=u_scale[:, cols], in0=norm_inv[:, cols], in1=log_len[:, cols], op=ALU.mult)
+
+        turned_u = {}
+        grouped_u = {}
+
+        def scale_and_turn(pair):
+            if not in_range(pair):
+                return
+            u_bf = stage.tile([P, 2, K], BF16)
+            for e in range(2):
+                t = 2 * pair + e
+                nc.vector.tensor_scalar(
+                    out=u_bf[:, e, :], in0=spatial(t), scalar1=u_scale[:, t : t + 1], scalar2=None,
+                    op0=ALU.mult,
+                )
+            turned_u[pair] = turn(u_bf[:])
+
+        def regroup_u(pair, by_vector):
+            if in_range(pair) and (pair - REGROUP_LEAD < OUT_LAG) == by_vector:
+                grouped_u[pair] = regroup(nc.vector.tensor_copy if by_vector else nc.scalar.copy, turned_u[pair])
+
+        def linear_map(h_psum, t):
+            cols = slice(t * P, (t + 1) * P)
+            nc.tensor.matmul_mx(
+                out=h_psum[:],
+                lhsT=u_codes[:, cols].bitcast(FP8X4),
+                lhsT_scale=u_scales[:, cols],
+                rhs=w_codes[:].bitcast(FP8X4),
+                rhs_scale=w_scales[:],
+                start=True,
+                stop=True,
+            )
+
+        first_h = {}
+        second_h = {}
+
+        def quantise_and_multiply(pair):
+            if not in_range(pair):
+                return
+            cols = slice(2 * pair * P, (2 * pair + 2) * P)
+            quantise(grouped_u[pair], u_codes[:, cols], u_scales[:, cols])
+            for t in (2 * pair, 2 * pair + 1):
+                h_first = psum_first.tile([P, N], F32)
+                linear_map(h_first, t)
+                first_h[t] = h_first
+
+        def multiply_again(pair):
+            if not in_range(pair):
+                return
+            for t in (2 * pair, 2 * pair + 1):
+                h_second = psum_second.tile([P, N], F32)
+                linear_map(h_second, t)
+                second_h[t] = h_second
+
+        def square_sum(pair):
+            if not in_range(pair):
+                return
+            for t in (2 * pair, 2 * pair + 1):
+                h_squares = unread.tile([P, N], BF16)
+                nc.scalar.activation(
+                    out=h_squares[:], in_=first_h[t][:], func=ACT.Square, accum_out=h_sq[:, t : t + 1]
+                )
+
+        def dot_with_bias(pair):
+            if not in_range(pair):
+                return
+            for t in (2 * pair, 2 * pair + 1):
+                h_times_bias = unread.tile([P, N], F32)
+                nc.vector.scalar_tensor_tensor(
+                    out=h_times_bias[:], in0=first_h[t][:], scalar=1.0, in1=bias_bf[:],
+                    op0=ALU.mult, op1=ALU.mult, accum_out=h_bias[:, t : t + 1],
+                )
+
+        def one_value(name):
+            return keep.tile([P, 1], F32, name=name)
+
+        bias_sq = one_value("bias_sq")
+        t_sq = one_value("t_sq")
+        t_raw = one_value("t_raw")
+        t_len = one_value("t_len")
+        grow_t = one_value("grow_t")
+        decay_t = one_value("decay_t")
+        two_cosh_t = one_value("two_cosh_t")
+        two_sinh_t = one_value("two_sinh_t")
+        cosh_t = one_value("cosh_t")
+        half_cosh_t = one_value("half_cosh_t")
+        t_inv = one_value("t_inv")
+        bias_factor = one_value("bias_factor")
+        half_bias_factor = one_value("half_bias_factor")
+        sinh_sq = one_value("sinh_sq")
+        cosh_sq = one_value("cosh_sq")
+        kappa = one_value("kappa")
+        bias_squares = keep.tile([P, N], F32)
+        scaled_bias = keep.tile([P, N], F32)
+
+        def bias_length():
+            nc.vector.scalar_tensor_tensor(
+                out=bias_squares[:], in0=bias_bf[:], scalar=1.0, in1=bias_bf[:],
+                op0=ALU.mult, op1=ALU.mult, accum_out=bias_sq[:],
+            )
+            nc.gpsimd.tensor_scalar(out=t_sq[:], in0=bias_sq[:], scalar1=1e-15, scalar2=None, op0=ALU.max)
+            nc.gpsimd.tensor_tensor(out=t_raw[:], in0=t_sq[:], in1=half[:, 0:1], op=ALU.pow)
+            nc.gpsimd.tensor_scalar(out=t_len[:], in0=t_raw[:], scalar1=1e-15, scalar2=15.0, op0=ALU.max, op1=ALU.min)
+
+        def bias_exponentials():
+            nc.scalar.activation(out=grow_t[:], in_=t_len[:], func=ACT.Exp)
+            nc.scalar.activation(out=decay_t[:], in_=t_len[:], func=ACT.Exp, scale=-1.0)
+
+        def bias_factors():
+            nc.vector.tensor_tensor(out=two_cosh_t[:], in0=grow_t[:], in1=decay_t[:], op=ALU.add)
+            nc.vector.tensor_tensor(out=two_sinh_t[:], in0=grow_t[:], in1=decay_t[:], op=ALU.subtract)
+            nc.vector.reciprocal(out=t_inv[:], in_=t_len[:])
+            nc.vector.tensor_scalar(out=cosh_t[:], in0=two_cosh_t[:], scalar1=0.5, scalar2=None, op0=ALU.mult)
+            nc.vector.tensor_scalar(out=half_cosh_t[:], in0=two_cosh_t[:], scalar1=0.25, scalar2=None, op0=ALU.mult)
+            nc.vector.scalar_tensor_tensor(
+                out=bias_factor[:], in0=two_sinh_t[:], scalar=0.5, in1=t_inv[:], op0=ALU.mult, op1=ALU.mult
+            )
+            nc.vector.tensor_tensor(out=cosh_sq[:], in0=cosh_t[:], in1=cosh_t[:], op=ALU.mult)
+            nc.vector.tensor_scalar(
+                out=half_bias_factor[:], in0=bias_factor[:], scalar1=0.5, scalar2=None, op0=ALU.mult
+            )
+            nc.vector.scalar_tensor_tensor(
+                out=sinh_sq[:], in0=bias_factor[:], scalar=bias_factor[:, 0:1], in1=bias_sq[:],
+                op0=ALU.mult, op1=ALU.mult,
+            )
+            nc.vector.tensor_scalar(
+                out=scaled_bias[:], in0=bias_bf[:], scalar1=bias_factor[:, 0:1], scalar2=None, op0=ALU.mult
+            )
+            nc.vector.scalar_tensor_tensor(
+                out=kappa[:], in0=sinh_sq[:], scalar=1.0, in1=cosh_sq[:], op0=ALU.add, op1=ALU.subtract
+            )
+
+        def inverse_length_of_h(c):
+            if c is None:
+                return
+            cols = chunk_columns(c)
+            nc.gpsimd.tensor_scalar(out=r_sq[:, cols], in0=h_sq[:, cols], scalar1=1e-30, scalar2=None, op0=ALU.max)
+            nc.gpsimd.tensor_tensor(out=r_inv[:, cols], in0=r_sq[:, cols], in1=minus_half[:], op=ALU.pow)
+
+        def length_of_h(c):
+            if c is None:
+                return
+            cols = chunk_columns(c)
+            nc.vector.tensor_tensor(out=r_len[:, cols], in0=r_sq[:, cols], in1=r_inv[:, cols], op=ALU.mult)
+            nc.vector.tensor_scalar(out=r_clamped[:, cols], in0=r_len[:, cols], scalar1=15.0, scalar2=None, op0=ALU.min)
+
+        def exponentials(c):
+            if c is None:
+                return
+            cols = chunk_columns(c)
+            nc.scalar.activation(out=grow[:, cols], in_=r_clamped[:, cols], func=ACT.Exp, scale=0.5)
+            nc.scalar.activation(out=decay[:, cols], in_=r_clamped[:, cols], func=ACT.Exp, scale=-0.5)
+
+        def factor_round_1(c):
+            if c is None:
+                return
+            cols = chunk_columns(c)
+            nc.vector.tensor_tensor(out=d[:, cols], in0=grow[:, cols], in1=decay[:, cols], op=ALU.subtract)
+            nc.vector.tensor_tensor(out=g2[:, cols], in0=grow[:, cols], in1=decay[:, cols], op=ALU.add)
+            nc.vector.scalar_tensor_tensor(
+                out=ca[:, cols], in0=h_bias[:, cols], scalar=half_bias_factor[:, 0:1], in1=r_inv[:, cols],
+                op0=ALU.mult, op1=ALU.mult,
+            )
+
+        def factor_round_2(c):
+            if c is None:
+                return
+            cols = chunk_columns(c)
+            nc.vector.tensor_tensor(out=ca_d[:, cols], in0=ca[:, cols], in1=d[:, cols], op=ALU.mult)
+            nc.vector.tensor_tensor(out=ca_g[:, cols], in0=ca[:, cols], in1=g2[:, cols], op=ALU.mult)
+            nc.vector.tensor_tensor(out=d_over_r[:, cols], in0=d[:, cols], in1=r_inv[:, cols], op=ALU.mult)
+
+        def factor_round_3(c):
+            if c is None:
+                return
+            cols = chunk_columns(c)
+            nc.vector.scalar_tensor_tensor(
+                out=inner_a[:, cols], in0=g2[:, cols], scalar=half_cosh_t[:, 0:1], in1=ca_d[:, cols],
+                op0=ALU.mult, op1=ALU.add,
+            )
+            nc.vector.scalar_tensor_tensor(
+                out=inner_w[:, cols], in0=d[:, cols], scalar=half_cosh_t[:, 0:1], in1=ca_g[:, cols],
+                op0=ALU.mult, op1=ALU.add,
+            )
+
+        def factor_round_4(c):
+            if c is None:
+                return
+            cols = chunk_columns(c)
+            nc.vector.tensor_tensor(out=h_factor[:, cols], in0=inner_a[:, cols], in1=d_over_r[:, cols], op=ALU.mult)
+            nc.vector.tensor_tensor(out=w_less_ct[:, cols], in0=inner_w[:, cols], in1=d[:, cols], op=ALU.mult)
+
+        def time_coordinate(c):
+            if c is None:
+                return
+            cols = chunk_columns(c)
+            nc.scalar.activation(out=w_sq[:, cols], in_=w_less_ct[:, cols], func=ACT.Square, bias=cosh_t[:, 0:1])
+            nc.gpsimd.tensor_scalar(
+                out=time_sq[:, cols], in0=w_sq[:, cols], scalar1=kappa[:, 0:1], scalar2=None, op0=ALU.add
+            )
+            nc.gpsimd.tensor_tensor(out=out_time[:, cols], in0=time_sq[:, cols], in1=half[:], op=ALU.pow)
+
+        rows_of_chunk = {}
+
+        def output_rows(pair):
+            if not in_range(pair):
+                return
+            c = pair // PAIRS_IN_CHUNK
+            if pair % PAIRS_IN_CHUNK == 0:
+                rows_sb = result.tile([P, CHUNK, WIDTH], F32)
+                rows_of_chunk[c] = rows_sb
+            for t in (2 * pair, 2 * pair + 1):
+                nc.vector.scalar_tensor_tensor(
+                    out=rows_of_chunk[c][:, t % CHUNK, 1:WIDTH], in0=second_h[t][:], scalar=h_factor[:, t : t + 1],
+                    in1=scaled_bias[:], op0=ALU.mult, op1=ALU.add,
+                )
+            if chunk_ended(pair) is not None:
+                nc.vector.tensor_copy(out=rows_of_chunk[c][:, :, 0], in_=out_time[:, chunk_columns(c)])
+                nc.sync.dma_start(out=out_rows[:, chunk_columns(c), :], in_=rows_of_chunk[c][:])
+
+        log_argument(0)
+        for i in range(0, PACK, 2):
+            cols = slice(i * P, (i + 2) * P)
+            quantise(regroup(nc.vector.tensor_copy, turn(w_sb[:, i : i + 2, :])), w_codes[:, cols], w_scales[:, cols])
+
+        for step in range(FIRST_STEP, LAST_STEP):
+            square_sum(step)
+            norm_square(step + NORM_LEAD)
+            regroup_u(step + REGROUP_LEAD, False)
+            if step == -SCALE_LEAD:
+                log_length(0)
+            if 1 <= step + 1 < CHUNKS:
+                log_length(step + 1)
+            if step == CHUNKS - 1:
+                bias_exponentials()
+            exponentials(chunk_ended(step - EXP_LAG))
+            time_coordinate(chunk_ended(step - FACTOR_LAG - 1))
+            scale_of_u(step + SCALE_LEAD)
+            dot_with_bias(step - DOT_LAG)
+            inverse_length_of_h(chunk_ended(step - DOT_LAG))
+            if step == CHUNKS:
+                bias_factors()
+            factor_round_1(chunk_ended(step - FACTOR_LAG))
+            quantise_and_multiply(step + QUANT_LEAD)
+            factor_round_2(chunk_ended(step - FACTOR_LAG))
+            output_rows(step - OUT_LAG)
+            multiply_again(step - OUT_LAG + 1)
+            length_of_h(chunk_ended(step - LENGTH_LAG))
+            factor_round_3(chunk_ended(step - FACTOR_LAG))
+            regroup_u(step + REGROUP_LEAD, True)
+            scale_and_turn(step + SCALE_LEAD)
+            factor_round_4(chunk_ended(step - FACTOR_LAG))
+            if 1 <= step + 2 < CHUNKS:
+                log_argument(step + 2)
+            if step == 1:
+                bias_length()

@@ -28,6 +28,7 @@ PAIRS_IN_GROUP = GROUP // 2
 PAIRS_IN_CHUNK = CHUNK // 2
 
 NORM_LEAD = 8
+INVERSE_LEAD = 6
 SCALE_LEAD = 3
 REGROUP_LEAD = 2
 QUANT_LEAD = 1
@@ -90,6 +91,8 @@ def tile_hyperboliclinearhyperboloid_t_kernel(tc, x, weight, bias, out):
         minus_half = keep.tile([P, CHUNK], F32)
         nc.gpsimd.memset(half[:], 0.5)
         nc.gpsimd.memset(minus_half[:], -0.5)
+        table_warmer = keep.tile([P, 1], F32)
+        nc.scalar.activation(out=table_warmer[:], in_=half[:, 0:1], func=ACT.Ln)
 
         def row_values(name):
             return keep.tile([P, TILES], F32, name=name)
@@ -122,7 +125,7 @@ def tile_hyperboliclinearhyperboloid_t_kernel(tc, x, weight, bias, out):
         inner_w = row_values("inner_w")
         h_factor = row_values("h_factor")
         w_less_ct = row_values("w_less_ct")
-        w_sq = row_values("w_sq")
+        w_sq_less = row_values("w_sq_less")
         time_sq = row_values("time_sq")
         out_time = row_values("out_time")
 
@@ -166,7 +169,7 @@ def tile_hyperboliclinearhyperboloid_t_kernel(tc, x, weight, bias, out):
                 return pair // PAIRS_IN_CHUNK
             return None
 
-        def log_argument(c):
+        def root_argument(c):
             cols = chunk_columns(c)
             nc.vector.tensor_scalar(
                 out=above_one[:, cols].rearrange("p (g t) -> p g t", t=GROUP), in0=time_coordinates(c),
@@ -177,6 +180,9 @@ def tile_hyperboliclinearhyperboloid_t_kernel(tc, x, weight, bias, out):
                 op0=ALU.add, op1=ALU.mult,
             )
             nc.vector.tensor_scalar(out=theta[:, cols], in0=above_one[:, cols], scalar1=1.0, scalar2=None, op0=ALU.add)
+
+        def log_argument(c):
+            cols = chunk_columns(c)
             nc.gpsimd.tensor_tensor(out=root[:, cols], in0=root_arg[:, cols], in1=half[:], op=ALU.pow)
             nc.gpsimd.tensor_tensor(out=log_arg[:, cols], in0=theta[:, cols], in1=root[:, cols], op=ALU.add)
 
@@ -193,7 +199,7 @@ def tile_hyperboliclinearhyperboloid_t_kernel(tc, x, weight, bias, out):
                     out=squares[:], in_=spatial(t), func=ACT.Square, accum_out=norm_sq[:, t : t + 1]
                 )
 
-        def scale_of_u(pair):
+        def inverse_norm(pair):
             if not in_range(pair) or pair % PAIRS_IN_GROUP != 0:
                 return
             cols = slice(2 * pair, 2 * pair + GROUP)
@@ -203,7 +209,12 @@ def tile_hyperboliclinearhyperboloid_t_kernel(tc, x, weight, bias, out):
             nc.gpsimd.tensor_tensor(
                 out=norm_inv[:, cols], in0=floor_sq[:, cols], in1=minus_half[:, 0:GROUP], op=ALU.pow
             )
-            nc.gpsimd.tensor_tensor(out=u_scale[:, cols], in0=norm_inv[:, cols], in1=log_len[:, cols], op=ALU.mult)
+
+        def scale_of_u(pair):
+            if not in_range(pair) or pair % PAIRS_IN_GROUP != 0:
+                return
+            cols = slice(2 * pair, 2 * pair + GROUP)
+            nc.vector.tensor_tensor(out=u_scale[:, cols], in0=norm_inv[:, cols], in1=log_len[:, cols], op=ALU.mult)
 
         turned_u = {}
         grouped_u = {}
@@ -287,14 +298,12 @@ def tile_hyperboliclinearhyperboloid_t_kernel(tc, x, weight, bias, out):
         decay_t = one_value("decay_t")
         two_cosh_t = one_value("two_cosh_t")
         two_sinh_t = one_value("two_sinh_t")
-        cosh_t = one_value("cosh_t")
         half_cosh_t = one_value("half_cosh_t")
         t_inv = one_value("t_inv")
         bias_factor = one_value("bias_factor")
         half_bias_factor = one_value("half_bias_factor")
         sinh_sq = one_value("sinh_sq")
-        cosh_sq = one_value("cosh_sq")
-        kappa = one_value("kappa")
+        time_base = one_value("time_base")
         bias_squares = keep.tile([P, N], F32)
         scaled_bias = keep.tile([P, N], F32)
 
@@ -315,12 +324,10 @@ def tile_hyperboliclinearhyperboloid_t_kernel(tc, x, weight, bias, out):
             nc.vector.tensor_tensor(out=two_cosh_t[:], in0=grow_t[:], in1=decay_t[:], op=ALU.add)
             nc.vector.tensor_tensor(out=two_sinh_t[:], in0=grow_t[:], in1=decay_t[:], op=ALU.subtract)
             nc.vector.reciprocal(out=t_inv[:], in_=t_len[:])
-            nc.vector.tensor_scalar(out=cosh_t[:], in0=two_cosh_t[:], scalar1=0.5, scalar2=None, op0=ALU.mult)
             nc.vector.tensor_scalar(out=half_cosh_t[:], in0=two_cosh_t[:], scalar1=0.25, scalar2=None, op0=ALU.mult)
             nc.vector.scalar_tensor_tensor(
                 out=bias_factor[:], in0=two_sinh_t[:], scalar=0.5, in1=t_inv[:], op0=ALU.mult, op1=ALU.mult
             )
-            nc.vector.tensor_tensor(out=cosh_sq[:], in0=cosh_t[:], in1=cosh_t[:], op=ALU.mult)
             nc.vector.tensor_scalar(
                 out=half_bias_factor[:], in0=bias_factor[:], scalar1=0.5, scalar2=None, op0=ALU.mult
             )
@@ -331,9 +338,7 @@ def tile_hyperboliclinearhyperboloid_t_kernel(tc, x, weight, bias, out):
             nc.vector.tensor_scalar(
                 out=scaled_bias[:], in0=bias_bf[:], scalar1=bias_factor[:, 0:1], scalar2=None, op0=ALU.mult
             )
-            nc.vector.scalar_tensor_tensor(
-                out=kappa[:], in0=sinh_sq[:], scalar=1.0, in1=cosh_sq[:], op0=ALU.add, op1=ALU.subtract
-            )
+            nc.vector.tensor_scalar(out=time_base[:], in0=sinh_sq[:], scalar1=1.0, scalar2=None, op0=ALU.add)
 
         def inverse_length_of_h(c):
             if c is None:
@@ -399,9 +404,12 @@ def tile_hyperboliclinearhyperboloid_t_kernel(tc, x, weight, bias, out):
             if c is None:
                 return
             cols = chunk_columns(c)
-            nc.scalar.activation(out=w_sq[:, cols], in_=w_less_ct[:, cols], func=ACT.Square, bias=cosh_t[:, 0:1])
+            nc.vector.scalar_tensor_tensor(
+                out=w_sq_less[:, cols], in0=w_less_ct[:, cols], scalar=two_cosh_t[:, 0:1], in1=w_less_ct[:, cols],
+                op0=ALU.add, op1=ALU.mult,
+            )
             nc.gpsimd.tensor_scalar(
-                out=time_sq[:, cols], in0=w_sq[:, cols], scalar1=kappa[:, 0:1], scalar2=None, op0=ALU.add
+                out=time_sq[:, cols], in0=w_sq_less[:, cols], scalar1=time_base[:, 0:1], scalar2=None, op0=ALU.add
             )
             nc.gpsimd.tensor_tensor(out=out_time[:, cols], in0=time_sq[:, cols], in1=half[:], op=ALU.pow)
 
@@ -423,39 +431,43 @@ def tile_hyperboliclinearhyperboloid_t_kernel(tc, x, weight, bias, out):
                 nc.vector.tensor_copy(out=rows_of_chunk[c][:, :, 0], in_=out_time[:, chunk_columns(c)])
                 nc.sync.dma_start(out=out_rows[:, chunk_columns(c), :], in_=rows_of_chunk[c][:])
 
+        root_argument(0)
         log_argument(0)
         for i in range(0, PACK, 2):
             cols = slice(i * P, (i + 2) * P)
             quantise(regroup(nc.vector.tensor_copy, turn(w_sb[:, i : i + 2, :])), w_codes[:, cols], w_scales[:, cols])
 
         for step in range(FIRST_STEP, LAST_STEP):
-            square_sum(step)
-            norm_square(step + NORM_LEAD)
-            regroup_u(step + REGROUP_LEAD, False)
-            if step == -SCALE_LEAD:
-                log_length(0)
-            if 1 <= step + 1 < CHUNKS:
-                log_length(step + 1)
+            inverse_length_of_h(chunk_ended(step - 1))
+            inverse_norm(step + INVERSE_LEAD)
+            if 1 <= step + 2 < CHUNKS:
+                log_argument(step + 2)
             if step == CHUNKS - 1:
                 bias_exponentials()
             exponentials(chunk_ended(step - EXP_LAG))
+            square_sum(step)
+            norm_square(step + NORM_LEAD)
+            regroup_u(step + REGROUP_LEAD, False)
+            if step == -SCALE_LEAD - 1:
+                log_length(0)
+            if 1 <= step + 1 < CHUNKS:
+                log_length(step + 1)
             time_coordinate(chunk_ended(step - FACTOR_LAG - 1))
             scale_of_u(step + SCALE_LEAD)
             dot_with_bias(step - DOT_LAG)
-            inverse_length_of_h(chunk_ended(step - DOT_LAG))
             if step == CHUNKS:
                 bias_factors()
             factor_round_1(chunk_ended(step - FACTOR_LAG))
             quantise_and_multiply(step + QUANT_LEAD)
             factor_round_2(chunk_ended(step - FACTOR_LAG))
-            output_rows(step - OUT_LAG)
-            multiply_again(step - OUT_LAG + 1)
             length_of_h(chunk_ended(step - LENGTH_LAG))
-            factor_round_3(chunk_ended(step - FACTOR_LAG))
             regroup_u(step + REGROUP_LEAD, True)
             scale_and_turn(step + SCALE_LEAD)
+            factor_round_3(chunk_ended(step - FACTOR_LAG))
+            output_rows(step - OUT_LAG)
+            multiply_again(step - OUT_LAG + 1)
             factor_round_4(chunk_ended(step - FACTOR_LAG))
-            if 1 <= step + 2 < CHUNKS:
-                log_argument(step + 2)
+            if 1 <= step + 3 < CHUNKS:
+                root_argument(step + 3)
             if step == 1:
                 bias_length()

@@ -22,10 +22,12 @@ PAIRS = TILES // 2
 GROUP = 4
 GROUP_PITCH = 2064
 CHUNK = 8
+ROUND = 16
 GROUPS = TILES // GROUP
 CHUNKS = TILES // CHUNK
 PAIRS_IN_GROUP = GROUP // 2
 PAIRS_IN_CHUNK = CHUNK // 2
+PAIRS_IN_ROUND = ROUND // 2
 
 NORM_LEAD = 8
 INVERSE_LEAD = 6
@@ -33,10 +35,11 @@ SCALE_LEAD = 3
 REGROUP_LEAD = 2
 QUANT_LEAD = 1
 DOT_LAG = 1
-LENGTH_LAG = 2
+LENGTH_LAG = 1
 EXP_LAG = 4
 FACTOR_LAG = 5
-OUT_LAG = 9
+OUT_LAG = PAIRS_IN_ROUND + FACTOR_LAG
+FIRST_EXP = PAIRS_IN_ROUND - 1 + EXP_LAG
 FIRST_STEP = -NORM_LEAD
 LAST_STEP = PAIRS + OUT_LAG
 
@@ -87,8 +90,8 @@ def tile_hyperboliclinearhyperboloid_t_kernel(tc, x, weight, bias, out):
 
         ident = keep.tile([P, P], BF16)
         make_identity(nc, ident[:])
-        half = keep.tile([P, CHUNK], F32)
-        minus_half = keep.tile([P, CHUNK], F32)
+        half = keep.tile([P, ROUND], F32)
+        minus_half = keep.tile([P, ROUND], F32)
         nc.gpsimd.memset(half[:], 0.5)
         nc.gpsimd.memset(minus_half[:], -0.5)
         table_warmer = keep.tile([P, 1], F32)
@@ -117,20 +120,27 @@ def tile_hyperboliclinearhyperboloid_t_kernel(tc, x, weight, bias, out):
         decay = row_values("decay")
         d = row_values("d")
         g2 = row_values("g2")
+        ca_r = row_values("ca_r")
         ca = row_values("ca")
         ca_d = row_values("ca_d")
         ca_g = row_values("ca_g")
         d_over_r = row_values("d_over_r")
+        ct_g = row_values("ct_g")
+        ct_d = row_values("ct_d")
         inner_a = row_values("inner_a")
         inner_w = row_values("inner_w")
         h_factor = row_values("h_factor")
         w_less_ct = row_values("w_less_ct")
+        w_plus_ct = row_values("w_plus_ct")
         w_sq_less = row_values("w_sq_less")
         time_sq = row_values("time_sq")
         out_time = row_values("out_time")
 
         def chunk_columns(c):
             return slice(c * CHUNK, (c + 1) * CHUNK)
+
+        def round_columns(c):
+            return slice(c * ROUND, (c + 1) * ROUND)
 
         u_codes = keep.tile([P, TILES * P], U32, align_bytes=64)
         u_scales = keep.tile([P, TILES * P], U8, align_bytes=64)
@@ -164,9 +174,9 @@ def tile_hyperboliclinearhyperboloid_t_kernel(tc, x, weight, bias, out):
         def in_range(pair):
             return 0 <= pair < PAIRS
 
-        def chunk_ended(pair):
-            if in_range(pair) and pair % PAIRS_IN_CHUNK == PAIRS_IN_CHUNK - 1:
-                return pair // PAIRS_IN_CHUNK
+        def round_ended(pair):
+            if in_range(pair) and pair % PAIRS_IN_ROUND == PAIRS_IN_ROUND - 1:
+                return pair // PAIRS_IN_ROUND
             return None
 
         def root_argument(c):
@@ -183,7 +193,7 @@ def tile_hyperboliclinearhyperboloid_t_kernel(tc, x, weight, bias, out):
 
         def log_argument(c):
             cols = chunk_columns(c)
-            nc.gpsimd.tensor_tensor(out=root[:, cols], in0=root_arg[:, cols], in1=half[:], op=ALU.pow)
+            nc.gpsimd.tensor_tensor(out=root[:, cols], in0=root_arg[:, cols], in1=half[:, 0:CHUNK], op=ALU.pow)
             nc.gpsimd.tensor_tensor(out=log_arg[:, cols], in0=theta[:, cols], in1=root[:, cols], op=ALU.add)
 
         def log_length(c):
@@ -232,7 +242,7 @@ def tile_hyperboliclinearhyperboloid_t_kernel(tc, x, weight, bias, out):
             turned_u[pair] = turn(u_bf[:])
 
         def regroup_u(pair, by_vector):
-            if in_range(pair) and (pair - REGROUP_LEAD < OUT_LAG) == by_vector:
+            if in_range(pair) and (pair < OUT_LAG) == by_vector:
                 grouped_u[pair] = regroup(nc.vector.tensor_copy if by_vector else nc.scalar.copy, turned_u[pair])
 
         def linear_map(h_psum, t):
@@ -340,77 +350,58 @@ def tile_hyperboliclinearhyperboloid_t_kernel(tc, x, weight, bias, out):
             )
             nc.vector.tensor_scalar(out=time_base[:], in0=sinh_sq[:], scalar1=1.0, scalar2=None, op0=ALU.add)
 
-        def inverse_length_of_h(c):
-            if c is None:
-                return
-            cols = chunk_columns(c)
-            nc.gpsimd.tensor_scalar(out=r_sq[:, cols], in0=h_sq[:, cols], scalar1=1e-30, scalar2=None, op0=ALU.max)
-            nc.gpsimd.tensor_tensor(out=r_inv[:, cols], in0=r_sq[:, cols], in1=minus_half[:], op=ALU.pow)
+        def row_product(result_values, left, right, cols):
+            nc.gpsimd.tensor_tensor(out=result_values[:, cols], in0=left[:, cols], in1=right[:, cols], op=ALU.mult)
+
+        def row_sum(result_values, left, right, cols):
+            nc.gpsimd.tensor_tensor(out=result_values[:, cols], in0=left[:, cols], in1=right[:, cols], op=ALU.add)
+
+        def row_scaled(result_values, values, factor, cols):
+            nc.gpsimd.tensor_scalar(
+                out=result_values[:, cols], in0=values[:, cols], scalar1=factor[:, 0:1], scalar2=None, op0=ALU.mult
+            )
+
+        def row_shifted(result_values, values, shift, cols):
+            nc.gpsimd.tensor_scalar(
+                out=result_values[:, cols], in0=values[:, cols], scalar1=shift[:, 0:1], scalar2=None, op0=ALU.add
+            )
 
         def length_of_h(c):
             if c is None:
                 return
-            cols = chunk_columns(c)
-            nc.vector.tensor_tensor(out=r_len[:, cols], in0=r_sq[:, cols], in1=r_inv[:, cols], op=ALU.mult)
-            nc.vector.tensor_scalar(out=r_clamped[:, cols], in0=r_len[:, cols], scalar1=15.0, scalar2=None, op0=ALU.min)
+            cols = round_columns(c)
+            nc.gpsimd.tensor_scalar(out=r_sq[:, cols], in0=h_sq[:, cols], scalar1=1e-30, scalar2=None, op0=ALU.max)
+            nc.gpsimd.tensor_tensor(out=r_inv[:, cols], in0=r_sq[:, cols], in1=minus_half[:], op=ALU.pow)
+            row_product(r_len, r_sq, r_inv, cols)
+            nc.gpsimd.tensor_scalar(out=r_clamped[:, cols], in0=r_len[:, cols], scalar1=15.0, scalar2=None, op0=ALU.min)
 
         def exponentials(c):
             if c is None:
                 return
-            cols = chunk_columns(c)
+            cols = round_columns(c)
             nc.scalar.activation(out=grow[:, cols], in_=r_clamped[:, cols], func=ACT.Exp, scale=0.5)
             nc.scalar.activation(out=decay[:, cols], in_=r_clamped[:, cols], func=ACT.Exp, scale=-0.5)
 
-        def factor_round_1(c):
+        def factor_of_h(c):
             if c is None:
                 return
-            cols = chunk_columns(c)
-            nc.vector.tensor_tensor(out=d[:, cols], in0=grow[:, cols], in1=decay[:, cols], op=ALU.subtract)
-            nc.vector.tensor_tensor(out=g2[:, cols], in0=grow[:, cols], in1=decay[:, cols], op=ALU.add)
-            nc.vector.scalar_tensor_tensor(
-                out=ca[:, cols], in0=h_bias[:, cols], scalar=half_bias_factor[:, 0:1], in1=r_inv[:, cols],
-                op0=ALU.mult, op1=ALU.mult,
-            )
-
-        def factor_round_2(c):
-            if c is None:
-                return
-            cols = chunk_columns(c)
-            nc.vector.tensor_tensor(out=ca_d[:, cols], in0=ca[:, cols], in1=d[:, cols], op=ALU.mult)
-            nc.vector.tensor_tensor(out=ca_g[:, cols], in0=ca[:, cols], in1=g2[:, cols], op=ALU.mult)
-            nc.vector.tensor_tensor(out=d_over_r[:, cols], in0=d[:, cols], in1=r_inv[:, cols], op=ALU.mult)
-
-        def factor_round_3(c):
-            if c is None:
-                return
-            cols = chunk_columns(c)
-            nc.vector.scalar_tensor_tensor(
-                out=inner_a[:, cols], in0=g2[:, cols], scalar=half_cosh_t[:, 0:1], in1=ca_d[:, cols],
-                op0=ALU.mult, op1=ALU.add,
-            )
-            nc.vector.scalar_tensor_tensor(
-                out=inner_w[:, cols], in0=d[:, cols], scalar=half_cosh_t[:, 0:1], in1=ca_g[:, cols],
-                op0=ALU.mult, op1=ALU.add,
-            )
-
-        def factor_round_4(c):
-            if c is None:
-                return
-            cols = chunk_columns(c)
-            nc.vector.tensor_tensor(out=h_factor[:, cols], in0=inner_a[:, cols], in1=d_over_r[:, cols], op=ALU.mult)
-            nc.vector.tensor_tensor(out=w_less_ct[:, cols], in0=inner_w[:, cols], in1=d[:, cols], op=ALU.mult)
-
-        def time_coordinate(c):
-            if c is None:
-                return
-            cols = chunk_columns(c)
-            nc.vector.scalar_tensor_tensor(
-                out=w_sq_less[:, cols], in0=w_less_ct[:, cols], scalar=two_cosh_t[:, 0:1], in1=w_less_ct[:, cols],
-                op0=ALU.add, op1=ALU.mult,
-            )
-            nc.gpsimd.tensor_scalar(
-                out=time_sq[:, cols], in0=w_sq_less[:, cols], scalar1=time_base[:, 0:1], scalar2=None, op0=ALU.add
-            )
+            cols = round_columns(c)
+            nc.gpsimd.tensor_tensor(out=d[:, cols], in0=grow[:, cols], in1=decay[:, cols], op=ALU.subtract)
+            row_sum(g2, grow, decay, cols)
+            row_scaled(ca_r, h_bias, half_bias_factor, cols)
+            row_product(ca, ca_r, r_inv, cols)
+            row_product(ca_d, ca, d, cols)
+            row_scaled(ct_g, g2, half_cosh_t, cols)
+            row_sum(inner_a, ct_g, ca_d, cols)
+            row_product(d_over_r, d, r_inv, cols)
+            row_product(h_factor, inner_a, d_over_r, cols)
+            row_product(ca_g, ca, g2, cols)
+            row_scaled(ct_d, d, half_cosh_t, cols)
+            row_sum(inner_w, ct_d, ca_g, cols)
+            row_product(w_less_ct, inner_w, d, cols)
+            row_shifted(w_plus_ct, w_less_ct, two_cosh_t, cols)
+            row_product(w_sq_less, w_less_ct, w_plus_ct, cols)
+            row_shifted(time_sq, w_sq_less, time_base, cols)
             nc.gpsimd.tensor_tensor(out=out_time[:, cols], in0=time_sq[:, cols], in1=half[:], op=ALU.pow)
 
         rows_of_chunk = {}
@@ -427,7 +418,7 @@ def tile_hyperboliclinearhyperboloid_t_kernel(tc, x, weight, bias, out):
                     out=rows_of_chunk[c][:, t % CHUNK, 1:WIDTH], in0=second_h[t][:], scalar=h_factor[:, t : t + 1],
                     in1=scaled_bias[:], op0=ALU.mult, op1=ALU.add,
                 )
-            if chunk_ended(pair) is not None:
+            if pair % PAIRS_IN_CHUNK == PAIRS_IN_CHUNK - 1:
                 nc.vector.tensor_copy(out=rows_of_chunk[c][:, :, 0], in_=out_time[:, chunk_columns(c)])
                 nc.sync.dma_start(out=out_rows[:, chunk_columns(c), :], in_=rows_of_chunk[c][:])
 
@@ -437,14 +428,16 @@ def tile_hyperboliclinearhyperboloid_t_kernel(tc, x, weight, bias, out):
             cols = slice(i * P, (i + 2) * P)
             quantise(regroup(nc.vector.tensor_copy, turn(w_sb[:, i : i + 2, :])), w_codes[:, cols], w_scales[:, cols])
 
+        assert CHUNKS - 1 <= FIRST_EXP
         for step in range(FIRST_STEP, LAST_STEP):
-            inverse_length_of_h(chunk_ended(step - 1))
             inverse_norm(step + INVERSE_LEAD)
             if 1 <= step + 2 < CHUNKS:
                 log_argument(step + 2)
-            if step == CHUNKS - 1:
+            length_of_h(round_ended(step - LENGTH_LAG))
+            factor_of_h(round_ended(step - FACTOR_LAG))
+            if step == FIRST_EXP:
                 bias_exponentials()
-            exponentials(chunk_ended(step - EXP_LAG))
+            exponentials(round_ended(step - EXP_LAG))
             square_sum(step)
             norm_square(step + NORM_LEAD)
             regroup_u(step + REGROUP_LEAD, False)
@@ -452,21 +445,15 @@ def tile_hyperboliclinearhyperboloid_t_kernel(tc, x, weight, bias, out):
                 log_length(0)
             if 1 <= step + 1 < CHUNKS:
                 log_length(step + 1)
-            time_coordinate(chunk_ended(step - FACTOR_LAG - 1))
             scale_of_u(step + SCALE_LEAD)
             dot_with_bias(step - DOT_LAG)
-            if step == CHUNKS:
+            if step == FIRST_EXP:
                 bias_factors()
-            factor_round_1(chunk_ended(step - FACTOR_LAG))
             quantise_and_multiply(step + QUANT_LEAD)
-            factor_round_2(chunk_ended(step - FACTOR_LAG))
-            length_of_h(chunk_ended(step - LENGTH_LAG))
             regroup_u(step + REGROUP_LEAD, True)
             scale_and_turn(step + SCALE_LEAD)
-            factor_round_3(chunk_ended(step - FACTOR_LAG))
             output_rows(step - OUT_LAG)
             multiply_again(step - OUT_LAG + 1)
-            factor_round_4(chunk_ended(step - FACTOR_LAG))
             if 1 <= step + 3 < CHUNKS:
                 root_argument(step + 3)
             if step == 1:

@@ -28,6 +28,7 @@ CHUNKS = TILES // CHUNK
 PAIRS_IN_GROUP = GROUP // 2
 PAIRS_IN_CHUNK = CHUNK // 2
 PAIRS_IN_ROUND = ROUND // 2
+PAIR_BLOCKS = 2 * WIDTH * 4 // 32 * 32 // 4
 
 NORM_LEAD = 8
 INVERSE_LEAD = 6
@@ -75,9 +76,9 @@ def tile_hyperboliclinearhyperboloid_t_kernel(tc, x, weight, bias, out):
             first = (t % GROUP) * WIDTH
             return x_sb[:, t // GROUP, first + 1 : first + WIDTH]
 
-        def time_coordinates(c):
-            groups = slice(c * CHUNK // GROUP, (c + 1) * CHUNK // GROUP)
-            return x_sb[:, groups, 0 : GROUP * WIDTH].rearrange("p g (t c) -> p g t c", c=WIDTH)[:, :, :, 0]
+        def time_coordinates(first_group, groups):
+            loads = x_sb[:, first_group : first_group + groups, 0 : GROUP * WIDTH]
+            return loads.rearrange("p g (t c) -> p g t c", c=WIDTH)[:, :, :, 0]
 
         load_group(0)
         nc.sync.dma_start(out=w_sb[:], in_=weight.rearrange("(i p) k -> p i k", p=P))
@@ -179,10 +180,14 @@ def tile_hyperboliclinearhyperboloid_t_kernel(tc, x, weight, bias, out):
                 return pair // PAIRS_IN_ROUND
             return None
 
-        def root_argument(c):
-            cols = chunk_columns(c)
+        def group_columns(first_group, groups):
+            return slice(first_group * GROUP, (first_group + groups) * GROUP)
+
+        def root_argument(first_group, groups):
+            cols = group_columns(first_group, groups)
             nc.vector.tensor_scalar(
-                out=above_one[:, cols].rearrange("p (g t) -> p g t", t=GROUP), in0=time_coordinates(c),
+                out=above_one[:, cols].rearrange("p (g t) -> p g t", t=GROUP),
+                in0=time_coordinates(first_group, groups),
                 scalar1=-1.0, scalar2=1e-7, op0=ALU.add, op1=ALU.max,
             )
             nc.vector.scalar_tensor_tensor(
@@ -191,13 +196,15 @@ def tile_hyperboliclinearhyperboloid_t_kernel(tc, x, weight, bias, out):
             )
             nc.vector.tensor_scalar(out=theta[:, cols], in0=above_one[:, cols], scalar1=1.0, scalar2=None, op0=ALU.add)
 
-        def log_argument(c):
-            cols = chunk_columns(c)
-            nc.gpsimd.tensor_tensor(out=root[:, cols], in0=root_arg[:, cols], in1=half[:, 0:CHUNK], op=ALU.pow)
+        def log_argument(first_group, groups):
+            cols = group_columns(first_group, groups)
+            nc.gpsimd.tensor_tensor(
+                out=root[:, cols], in0=root_arg[:, cols], in1=half[:, 0 : groups * GROUP], op=ALU.pow
+            )
             nc.gpsimd.tensor_tensor(out=log_arg[:, cols], in0=theta[:, cols], in1=root[:, cols], op=ALU.add)
 
-        def log_length(c):
-            cols = chunk_columns(c)
+        def log_length(first_group, groups):
+            cols = group_columns(first_group, groups)
             nc.scalar.activation(out=log_len[:, cols], in_=log_arg[:, cols], func=ACT.Ln)
 
         def norm_square(pair):
@@ -242,7 +249,7 @@ def tile_hyperboliclinearhyperboloid_t_kernel(tc, x, weight, bias, out):
             turned_u[pair] = turn(u_bf[:])
 
         def regroup_u(pair, by_vector):
-            if in_range(pair) and (pair < OUT_LAG) == by_vector:
+            if in_range(pair) and (pair - REGROUP_LEAD < OUT_LAG) == by_vector:
                 grouped_u[pair] = regroup(nc.vector.tensor_copy if by_vector else nc.scalar.copy, turned_u[pair])
 
         def linear_map(h_psum, t):
@@ -402,7 +409,9 @@ def tile_hyperboliclinearhyperboloid_t_kernel(tc, x, weight, bias, out):
             row_shifted(w_plus_ct, w_less_ct, two_cosh_t, cols)
             row_product(w_sq_less, w_less_ct, w_plus_ct, cols)
             row_shifted(time_sq, w_sq_less, time_base, cols)
-            nc.gpsimd.tensor_tensor(out=out_time[:, cols], in0=time_sq[:, cols], in1=half[:], op=ALU.pow)
+            for chunk in range(c * ROUND // CHUNK, (c + 1) * ROUND // CHUNK):
+                cols = chunk_columns(chunk)
+                nc.gpsimd.tensor_tensor(out=out_time[:, cols], in0=time_sq[:, cols], in1=half[:, 0:CHUNK], op=ALU.pow)
 
         rows_of_chunk = {}
 
@@ -410,7 +419,8 @@ def tile_hyperboliclinearhyperboloid_t_kernel(tc, x, weight, bias, out):
             if not in_range(pair):
                 return
             c = pair // PAIRS_IN_CHUNK
-            if pair % PAIRS_IN_CHUNK == 0:
+            place = pair % PAIRS_IN_CHUNK
+            if place == 0:
                 rows_sb = result.tile([P, CHUNK, WIDTH], F32)
                 rows_of_chunk[c] = rows_sb
             for t in (2 * pair, 2 * pair + 1):
@@ -418,21 +428,33 @@ def tile_hyperboliclinearhyperboloid_t_kernel(tc, x, weight, bias, out):
                     out=rows_of_chunk[c][:, t % CHUNK, 1:WIDTH], in0=second_h[t][:], scalar=h_factor[:, t : t + 1],
                     in1=scaled_bias[:], op0=ALU.mult, op1=ALU.add,
                 )
-            if pair % PAIRS_IN_CHUNK == PAIRS_IN_CHUNK - 1:
+            if place < PAIRS_IN_CHUNK - 2:
+                return
+            if place == PAIRS_IN_CHUNK - 2:
                 nc.vector.tensor_copy(out=rows_of_chunk[c][:, :, 0], in_=out_time[:, chunk_columns(c)])
-                nc.sync.dma_start(out=out_rows[:, chunk_columns(c), :], in_=rows_of_chunk[c][:])
+            cut = (PAIRS_IN_CHUNK - 1) * PAIR_BLOCKS
+            first = 0 if place == PAIRS_IN_CHUNK - 2 else cut
+            last = cut if place == PAIRS_IN_CHUNK - 2 else CHUNK * WIDTH
+            nc.sync.dma_start(
+                out=out_rows[:, chunk_columns(c), :].rearrange("p t c -> p (t c)")[:, first:last],
+                in_=rows_of_chunk[c][:].rearrange("p t c -> p (t c)")[:, first:last],
+            )
 
-        root_argument(0)
-        log_argument(0)
+        root_argument(0, 1)
+        log_argument(0, 1)
         for i in range(0, PACK, 2):
             cols = slice(i * P, (i + 2) * P)
             quantise(regroup(nc.vector.tensor_copy, turn(w_sb[:, i : i + 2, :])), w_codes[:, cols], w_scales[:, cols])
 
-        assert CHUNKS - 1 <= FIRST_EXP
+        log_step = {}
+        log_step[-SCALE_LEAD] = (1, 1)
+        for c in range(1, CHUNKS):
+            log_step[4 * (c - 1) // 3] = (2 * c, 2)
+        assert max(log_step) < FIRST_EXP
         for step in range(FIRST_STEP, LAST_STEP):
             inverse_norm(step + INVERSE_LEAD)
-            if 1 <= step + 2 < CHUNKS:
-                log_argument(step + 2)
+            if step + 1 in log_step:
+                log_argument(*log_step[step + 1])
             length_of_h(round_ended(step - LENGTH_LAG))
             factor_of_h(round_ended(step - FACTOR_LAG))
             if step == FIRST_EXP:
@@ -441,10 +463,10 @@ def tile_hyperboliclinearhyperboloid_t_kernel(tc, x, weight, bias, out):
             square_sum(step)
             norm_square(step + NORM_LEAD)
             regroup_u(step + REGROUP_LEAD, False)
-            if step == -SCALE_LEAD - 1:
-                log_length(0)
-            if 1 <= step + 1 < CHUNKS:
-                log_length(step + 1)
+            if step == FIRST_STEP + 1:
+                log_length(0, 1)
+            if step in log_step:
+                log_length(*log_step[step])
             scale_of_u(step + SCALE_LEAD)
             dot_with_bias(step - DOT_LAG)
             if step == FIRST_EXP:
@@ -454,7 +476,7 @@ def tile_hyperboliclinearhyperboloid_t_kernel(tc, x, weight, bias, out):
             scale_and_turn(step + SCALE_LEAD)
             output_rows(step - OUT_LAG)
             multiply_again(step - OUT_LAG + 1)
-            if 1 <= step + 3 < CHUNKS:
-                root_argument(step + 3)
+            if step + 2 in log_step:
+                root_argument(*log_step[step + 2])
             if step == 1:
                 bias_length()

from contextlib import ExitStack

import concourse.mybir as mybir
from concourse.masks import make_identity

F32 = mybir.dt.float32
BF16 = mybir.dt.bfloat16
U32 = mybir.dt.uint32
U8 = mybir.dt.uint8
FP8X4 = mybir.dt.float8_e4m3fn_x4
ALU = mybir.AluOpType
ACT = mybir.ActivationFunctionType

P = 128
PACK = 4
ROWS = 8192
K = 512
N = 512
WIDTH = K + 1
TILES = ROWS // P
PAIRS = TILES // 2
GROUP = 4
GROUP_PITCH = 2064
CHUNK = 8
ROUND = 16
GROUPS = TILES // GROUP
CHUNKS = TILES // CHUNK
PAIRS_IN_GROUP = GROUP // 2
PAIRS_IN_CHUNK = CHUNK // 2
PAIRS_IN_ROUND = ROUND // 2
PAIR_BLOCKS = 2 * WIDTH * 4 // 32 * 32 // 4

NORM_LEAD = 8
INVERSE_LEAD = 6
SCALE_LEAD = 3
REGROUP_LEAD = 2
QUANT_LEAD = 1
DOT_LAG = 1
LENGTH_LAG = 1
EXP_LAG = 4
FACTOR_LAG = 5
OUT_LAG = PAIRS_IN_ROUND + FACTOR_LAG
FIRST_EXP = PAIRS_IN_ROUND - 1 + EXP_LAG
FIRST_STEP = -NORM_LEAD
LAST_STEP = PAIRS + OUT_LAG

FLOPS = 2 * ROWS * K * N


def tile_hyperboliclinearhyperboloid_t_kernel(tc, x, weight, bias, out):
    nc = tc.nc
    x_rows = x.rearrange("(p t) c -> p t c", t=TILES)
    out_rows = out.rearrange("(p t) c -> p t c", t=TILES)

    with ExitStack() as ctx:
        ctx.enter_context(tc.manual_schedule())
        keep = ctx.enter_context(tc.tile_pool(name="keep", bufs=1))
        stage = ctx.enter_context(tc.tile_pool(name="stage", bufs=3))
        unread = ctx.enter_context(tc.tile_pool(name="unread", bufs=4))
        result = ctx.enter_context(tc.tile_pool(name="result", bufs=3))
        psum_turned = ctx.enter_context(tc.psum_pool(name="psum_turned", bufs=2))
        psum_first = ctx.enter_context(tc.psum_pool(name="psum_first", bufs=4))
        psum_second = ctx.enter_context(tc.psum_pool(name="psum_second", bufs=2))

        x_sb = keep.tile([P, GROUPS, GROUP_PITCH], BF16)
        w_sb = keep.tile([P, PACK, K], BF16)
        bias_bf = keep.tile([P, N], BF16)

        def load_group(g):
            tiles = slice(g * GROUP, (g + 1) * GROUP)
            nc.sync.dma_start(
                out=x_sb[:, g, 0 : GROUP * WIDTH], in_=x_rows[:, tiles, :].rearrange("p t c -> p (t c)")
            )

        def spatial(t):
            first = (t % GROUP) * WIDTH
            return x_sb[:, t // GROUP, first + 1 : first + WIDTH]

        def time_coordinates(first_group, groups):
            loads = x_sb[:, first_group : first_group + groups, 0 : GROUP * WIDTH]
            return loads.rearrange("p g (t c) -> p g t c", c=WIDTH)[:, :, :, 0]

        load_group(0)
        nc.sync.dma_start(out=w_sb[:], in_=weight.rearrange("(i p) k -> p i k", p=P))
        load_group(1)
        load_group(2)
        load_group(3)
        nc.sync.dma_start(out=bias_bf[:], in_=bias.rearrange("o n -> (o n)").partition_broadcast(P))
        for g in range(4, GROUPS):
            load_group(g)

        ident = keep.tile([P, P], BF16)
        make_identity(nc, ident[:])
        half = keep.tile([P, ROUND], F32)
        minus_half = keep.tile([P, ROUND], F32)
        nc.gpsimd.memset(half[:], 0.5)
        nc.gpsimd.memset(minus_half[:], -0.5)
        table_warmer = keep.tile([P, 1], F32)
        nc.scalar.activation(out=table_warmer[:], in_=half[:, 0:1], func=ACT.Ln)

        def row_values(name):
            return keep.tile([P, TILES], F32, name=name)

        above_one = row_values("above_one")
        theta = row_values("theta")
        root_arg = row_values("root_arg")
        root = row_values("root")
        log_arg = row_values("log_arg")
        log_len = row_values("log_len")
        norm_sq = row_values("norm_sq")
        floor_sq = row_values("floor_sq")
        norm_inv = row_values("norm_inv")
        u_scale = row_values("u_scale")
        h_sq = row_values("h_sq")
        h_bias = row_values("h_bias")
        r_sq = row_values("r_sq")
        r_inv = row_values("r_inv")
        r_len = row_values("r_len")
        r_clamped = row_values("r_clamped")
        grow = row_values("grow")
        decay = row_values("decay")
        d = row_values("d")
        g2 = row_values("g2")
        ca_r = row_values("ca_r")
        ca = row_values("ca")
        ca_d = row_values("ca_d")
        ca_g = row_values("ca_g")
        d_over_r = row_values("d_over_r")
        ct_g = row_values("ct_g")
        ct_d = row_values("ct_d")
        inner_a = row_values("inner_a")
        inner_w = row_values("inner_w")
        h_factor = row_values("h_factor")
        w_less_ct = row_values("w_less_ct")
        w_plus_ct = row_values("w_plus_ct")
        w_sq_less = row_values("w_sq_less")
        time_sq = row_values("time_sq")
        out_time = row_values("out_time")

        def chunk_columns(c):
            return slice(c * CHUNK, (c + 1) * CHUNK)

        def round_columns(c):
            return slice(c * ROUND, (c + 1) * ROUND)

        u_codes = keep.tile([P, TILES * P], U32, align_bytes=64)
        u_scales = keep.tile([P, TILES * P], U8, align_bytes=64)
        w_codes = keep.tile([P, N], U32, align_bytes=64)
        w_scales = keep.tile([P, N], U8, align_bytes=64)

        def turn(two_tiles):
            turned = psum_turned.tile([P, 2 * PACK, P], BF16)
            for e in range(2):
                for j in range(PACK):
                    nc.tensor.transpose(
                        out=turned[:, e * PACK + j, :],
                        in_=two_tiles[:, e, j * P : (j + 1) * P],
                        identity=ident[:],
                    )
            return turned

        def regroup(copy, turned):
            grouped = stage.tile([P, 2 * P, PACK], BF16, align_bytes=64)
            copy(
                out=grouped[:].rearrange("p (e r) j -> p e r j", e=2),
                in_=turned[:].rearrange("p (e j) r -> p e r j", e=2),
            )
            return grouped

        def quantise(grouped, codes, scales):
            nc.vector.quantize_mx(
                out=codes.bitcast(FP8X4), scales=scales, in_=grouped[:].rearrange("p r j -> p (r j)")
            )

        def in_range(pair):
            return 0 <= pair < PAIRS

        def round_ended(pair):
            if in_range(pair) and pair % PAIRS_IN_ROUND == PAIRS_IN_ROUND - 1:
                return pair // PAIRS_IN_ROUND
            return None

        def group_columns(first_group, groups):
            return slice(first_group * GROUP, (first_group + groups) * GROUP)

        def root_argument(first_group, groups):
            cols = group_columns(first_group, groups)
            nc.vector.tensor_scalar(
                out=above_one[:, cols].rearrange("p (g t) -> p g t", t=GROUP),
                in0=time_coordinates(first_group, groups),
                scalar1=-1.0, scalar2=1e-7, op0=ALU.add, op1=ALU.max,
            )
            nc.vector.scalar_tensor_tensor(
                out=root_arg[:, cols], in0=above_one[:, cols], scalar=2.0, in1=above_one[:, cols],
                op0=ALU.add, op1=ALU.mult,
            )
            nc.vector.tensor_scalar(out=theta[:, cols], in0=above_one[:, cols], scalar1=1.0, scalar2=None, op0=ALU.add)

        def log_argument(first_group, groups):
            cols = group_columns(first_group, groups)
            nc.gpsimd.tensor_tensor(
                out=root[:, cols], in0=root_arg[:, cols], in1=half[:, 0 : groups * GROUP], op=ALU.pow
            )
            nc.gpsimd.tensor_tensor(out=log_arg[:, cols], in0=theta[:, cols], in1=root[:, cols], op=ALU.add)

        def log_length(first_group, groups):
            cols = group_columns(first_group, groups)
            nc.scalar.activation(out=log_len[:, cols], in_=log_arg[:, cols], func=ACT.Ln)

        def norm_square(pair):
            if not in_range(pair):
                return
            for t in (2 * pair, 2 * pair + 1):
                squares = unread.tile([P, K], BF16)
                nc.scalar.activation(
                    out=squares[:], in_=spatial(t), func=ACT.Square, accum_out=norm_sq[:, t : t + 1]
                )

        def inverse_norm(pair):
            if not in_range(pair) or pair % PAIRS_IN_GROUP != 0:
                return
            cols = slice(2 * pair, 2 * pair + GROUP)
            nc.gpsimd.tensor_scalar(
                out=floor_sq[:, cols], in0=norm_sq[:, cols], scalar1=1e-30, scalar2=None, op0=ALU.max
            )
            nc.gpsimd.tensor_tensor(
                out=norm_inv[:, cols], in0=floor_sq[:, cols], in1=minus_half[:, 0:GROUP], op=ALU.pow
            )

        def scale_of_u(pair):
            if not in_range(pair) or pair % PAIRS_IN_GROUP != 0:
                return
            cols = slice(2 * pair, 2 * pair + GROUP)
            nc.vector.tensor_tensor(out=u_scale[:, cols], in0=norm_inv[:, cols], in1=log_len[:, cols], op=ALU.mult)

        turned_u = {}
        grouped_u = {}

        def scale_and_turn(pair):
            if not in_range(pair):
                return
            u_bf = stage.tile([P, 2, K], BF16)
            for e in range(2):
                t = 2 * pair + e
                nc.vector.tensor_scalar(
                    out=u_bf[:, e, :], in0=spatial(t), scalar1=u_scale[:, t : t + 1], scalar2=None,
                    op0=ALU.mult,
                )
            turned_u[pair] = turn(u_bf[:])

        def regroup_u(pair, by_vector):
            if in_range(pair) and (pair - REGROUP_LEAD < OUT_LAG) == by_vector:
                grouped_u[pair] = regroup(nc.vector.tensor_copy if by_vector else nc.scalar.copy, turned_u[pair])

        def linear_map(h_psum, t):
            cols = slice(t * P, (t + 1) * P)
            nc.tensor.matmul_mx(
                out=h_psum[:],
                lhsT=u_codes[:, cols].bitcast(FP8X4),
                lhsT_scale=u_scales[:, cols],
                rhs=w_codes[:].bitcast(FP8X4),
                rhs_scale=w_scales[:],
                start=True,
                stop=True,
            )

        first_h = {}
        second_h = {}

        def quantise_and_multiply(pair):
            if not in_range(pair):
                return
            cols = slice(2 * pair * P, (2 * pair + 2) * P)
            quantise(grouped_u[pair], u_codes[:, cols], u_scales[:, cols])
            for t in (2 * pair, 2 * pair + 1):
                h_first = psum_first.tile([P, N], F32)
                linear_map(h_first, t)
                first_h[t] = h_first

        def multiply_again(pair):
            if not in_range(pair):
                return
            for t in (2 * pair, 2 * pair + 1):
                h_second = psum_second.tile([P, N], F32)
                linear_map(h_second, t)
                second_h[t] = h_second

        def square_sum(pair):
            if not in_range(pair):
                return
            for t in (2 * pair, 2 * pair + 1):
                h_squares = unread.tile([P, N], BF16)
                nc.scalar.activation(
                    out=h_squares[:], in_=first_h[t][:], func=ACT.Square, accum_out=h_sq[:, t : t + 1]
                )

        def dot_with_bias(pair):
            if not in_range(pair):
                return
            for t in (2 * pair, 2 * pair + 1):
                h_times_bias = unread.tile([P, N], F32)
                nc.vector.scalar_tensor_tensor(
                    out=h_times_bias[:], in0=first_h[t][:], scalar=1.0, in1=bias_bf[:],
                    op0=ALU.mult, op1=ALU.mult, accum_out=h_bias[:, t : t + 1],
                )

        def one_value(name):
            return keep.tile([P, 1], F32, name=name)

        bias_sq = one_value("bias_sq")
        t_sq = one_value("t_sq")
        t_raw = one_value("t_raw")
        t_len = one_value("t_len")
        grow_t = one_value("grow_t")
        decay_t = one_value("decay_t")
        two_cosh_t = one_value("two_cosh_t")
        two_sinh_t = one_value("two_sinh_t")
        half_cosh_t = one_value("half_cosh_t")
        t_inv = one_value("t_inv")
        bias_factor = one_value("bias_factor")
        half_bias_factor = one_value("half_bias_factor")
        sinh_sq = one_value("sinh_sq")
        time_base = one_value("time_base")
        bias_squares = keep.tile([P, N], F32)
        scaled_bias = keep.tile([P, N], F32)

        def bias_length():
            nc.vector.scalar_tensor_tensor(
                out=bias_squares[:], in0=bias_bf[:], scalar=1.0, in1=bias_bf[:],
                op0=ALU.mult, op1=ALU.mult, accum_out=bias_sq[:],
            )
            nc.gpsimd.tensor_scalar(out=t_sq[:], in0=bias_sq[:], scalar1=1e-15, scalar2=None, op0=ALU.max)
            nc.gpsimd.tensor_tensor(out=t_raw[:], in0=t_sq[:], in1=half[:, 0:1], op=ALU.pow)
            nc.gpsimd.tensor_scalar(out=t_len[:], in0=t_raw[:], scalar1=1e-15, scalar2=15.0, op0=ALU.max, op1=ALU.min)

        def bias_exponentials():
            nc.scalar.activation(out=grow_t[:], in_=t_len[:], func=ACT.Exp)
            nc.scalar.activation(out=decay_t[:], in_=t_len[:], func=ACT.Exp, scale=-1.0)

        def bias_factors():
            nc.vector.tensor_tensor(out=two_cosh_t[:], in0=grow_t[:], in1=decay_t[:], op=ALU.add)
            nc.vector.tensor_tensor(out=two_sinh_t[:], in0=grow_t[:], in1=decay_t[:], op=ALU.subtract)
            nc.vector.reciprocal(out=t_inv[:], in_=t_len[:])
            nc.vector.tensor_scalar(out=half_cosh_t[:], in0=two_cosh_t[:], scalar1=0.25, scalar2=None, op0=ALU.mult)
            nc.vector.scalar_tensor_tensor(
                out=bias_factor[:], in0=two_sinh_t[:], scalar=0.5, in1=t_inv[:], op0=ALU.mult, op1=ALU.mult
            )
            nc.vector.tensor_scalar(
                out=half_bias_factor[:], in0=bias_factor[:], scalar1=0.5, scalar2=None, op0=ALU.mult
            )
            nc.vector.scalar_tensor_tensor(
                out=sinh_sq[:], in0=bias_factor[:], scalar=bias_factor[:, 0:1], in1=bias_sq[:],
                op0=ALU.mult, op1=ALU.mult,
            )
            nc.vector.tensor_scalar(
                out=scaled_bias[:], in0=bias_bf[:], scalar1=bias_factor[:, 0:1], scalar2=None, op0=ALU.mult
            )
            nc.vector.tensor_scalar(out=time_base[:], in0=sinh_sq[:], scalar1=1.0, scalar2=None, op0=ALU.add)

        def row_product(result_values, left, right, cols):
            nc.gpsimd.tensor_tensor(out=result_values[:, cols], in0=left[:, cols], in1=right[:, cols], op=ALU.mult)

        def row_sum(result_values, left, right, cols):
            nc.gpsimd.tensor_tensor(out=result_values[:, cols], in0=left[:, cols], in1=right[:, cols], op=ALU.add)

        def row_scaled(result_values, values, factor, cols):
            nc.gpsimd.tensor_scalar(
                out=result_values[:, cols], in0=values[:, cols], scalar1=factor[:, 0:1], scalar2=None, op0=ALU.mult
            )

        def row_shifted(result_values, values, shift, cols):
            nc.gpsimd.tensor_scalar(
                out=result_values[:, cols], in0=values[:, cols], scalar1=shift[:, 0:1], scalar2=None, op0=ALU.add
            )

        def length_of_h(c):
            if c is None:
                return
            cols = round_columns(c)
            nc.gpsimd.tensor_scalar(out=r_sq[:, cols], in0=h_sq[:, cols], scalar1=1e-30, scalar2=None, op0=ALU.max)
            nc.gpsimd.tensor_tensor(out=r_inv[:, cols], in0=r_sq[:, cols], in1=minus_half[:], op=ALU.pow)
            row_product(r_len, r_sq, r_inv, cols)
            nc.gpsimd.tensor_scalar(out=r_clamped[:, cols], in0=r_len[:, cols], scalar1=15.0, scalar2=None, op0=ALU.min)

        def exponentials(c):
            if c is None:
                return
            cols = round_columns(c)
            nc.scalar.activation(out=grow[:, cols], in_=r_clamped[:, cols], func=ACT.Exp, scale=0.5)
            nc.scalar.activation(out=decay[:, cols], in_=r_clamped[:, cols], func=ACT.Exp, scale=-0.5)

        def factor_of_h(c):
            if c is None:
                return
            cols = round_columns(c)
            nc.gpsimd.tensor_tensor(out=d[:, cols], in0=grow[:, cols], in1=decay[:, cols], op=ALU.subtract)
            row_sum(g2, grow, decay, cols)
            row_scaled(ca_r, h_bias, half_bias_factor, cols)
            row_product(ca, ca_r, r_inv, cols)
            row_product(ca_d, ca, d, cols)
            row_scaled(ct_g, g2, half_cosh_t, cols)
            row_sum(inner_a, ct_g, ca_d, cols)
            row_product(d_over_r, d, r_inv, cols)
            row_product(h_factor, inner_a, d_over_r, cols)
            row_product(ca_g, ca, g2, cols)
            row_scaled(ct_d, d, half_cosh_t, cols)
            row_sum(inner_w, ct_d, ca_g, cols)
            row_product(w_less_ct, inner_w, d, cols)
            row_shifted(w_plus_ct, w_less_ct, two_cosh_t, cols)
            row_product(w_sq_less, w_less_ct, w_plus_ct, cols)
            row_shifted(time_sq, w_sq_less, time_base, cols)
            for chunk in range(c * ROUND // CHUNK, (c + 1) * ROUND // CHUNK):
                cols = chunk_columns(chunk)
                nc.gpsimd.tensor_tensor(out=out_time[:, cols], in0=time_sq[:, cols], in1=half[:, 0:CHUNK], op=ALU.pow)

        rows_of_chunk = {}

        def output_rows(pair):
            if not in_range(pair):
                return
            c = pair // PAIRS_IN_CHUNK
            place = pair % PAIRS_IN_CHUNK
            if place == 0:
                rows_sb = result.tile([P, CHUNK, WIDTH], F32)
                rows_of_chunk[c] = rows_sb
            for t in (2 * pair, 2 * pair + 1):
                nc.vector.scalar_tensor_tensor(
                    out=rows_of_chunk[c][:, t % CHUNK, 1:WIDTH], in0=second_h[t][:], scalar=h_factor[:, t : t + 1],
                    in1=scaled_bias[:], op0=ALU.mult, op1=ALU.add,
                )
            if place < PAIRS_IN_CHUNK - 2:
                return
            if place == PAIRS_IN_CHUNK - 2:
                nc.vector.tensor_copy(out=rows_of_chunk[c][:, :, 0], in_=out_time[:, chunk_columns(c)])
            cut = (PAIRS_IN_CHUNK - 1) * PAIR_BLOCKS
            first = 0 if place == PAIRS_IN_CHUNK - 2 else cut
            last = cut if place == PAIRS_IN_CHUNK - 2 else CHUNK * WIDTH
            nc.sync.dma_start(
                out=out_rows[:, chunk_columns(c), :].rearrange("p t c -> p (t c)")[:, first:last],
                in_=rows_of_chunk[c][:].rearrange("p t c -> p (t c)")[:, first:last],
            )

        root_argument(0, 1)
        log_argument(0, 1)
        for i in range(0, PACK, 2):
            cols = slice(i * P, (i + 2) * P)
            quantise(regroup(nc.vector.tensor_copy, turn(w_sb[:, i : i + 2, :])), w_codes[:, cols], w_scales[:, cols])

        log_step = {}
        log_step[-SCALE_LEAD] = (1, 1)
        for c in range(1, CHUNKS):
            log_step[4 * (c - 1) // 3] = (2 * c, 2)
        assert max(log_step) < FIRST_EXP
        for step in range(FIRST_STEP, LAST_STEP):
            inverse_norm(step + INVERSE_LEAD)
            if step + 1 in log_step:
                log_argument(*log_step[step + 1])
            length_of_h(round_ended(step - LENGTH_LAG))
            factor_of_h(round_ended(step - FACTOR_LAG))
            if step == FIRST_EXP:
                bias_exponentials()
            exponentials(round_ended(step - EXP_LAG))
            square_sum(step)
            norm_square(step + NORM_LEAD)
            regroup_u(step + REGROUP_LEAD, False)
            if step == FIRST_STEP + 1:
                log_length(0, 1)
            if step in log_step:
                log_length(*log_step[step])
            scale_of_u(step + SCALE_LEAD)
            dot_with_bias(step - DOT_LAG)
            if step == FIRST_EXP:
                bias_factors()
            quantise_and_multiply(step + QUANT_LEAD)
            regroup_u(step + REGROUP_LEAD, True)
            scale_and_turn(step + SCALE_LEAD)
            output_rows(step - OUT_LAG)
            multiply_again(step - OUT_LAG + 1)
            if step + 2 in log_step:
                root_argument(*log_step[step + 2])
            if step == 1:
                bias_length()
